import numpy as np
import ml_dtypes


def mxq(x, axis, fmt="e4m3"):
    dtype, down = {"e4m3": (ml_dtypes.float8_e4m3fn, 7), "e5m2": (ml_dtypes.float8_e5m2, 14)}[fmt]
    v = np.moveaxis(np.asarray(x, np.float32).astype(ml_dtypes.bfloat16).astype(np.float64), axis, -1)
    blocks = v.reshape(v.shape[:-1] + (-1, 32))
    amax = np.abs(blocks).max(-1, keepdims=True)
    byte = np.maximum(np.where(amax > 0, np.frexp(amax)[1] - 1 + 127, 0) - down, 1)
    scale = np.exp2(byte - 127.0)
    codes = (blocks / scale).astype(np.float32).astype(dtype).astype(np.float64)
    return np.moveaxis((codes * scale).reshape(v.shape), -1, axis)


WIDE = False


def mx_kscale(k):
    if not WIDE:
        return np.ones(k)
    levels = np.array([10, -10, 5, -5, 0])
    a = np.random.permutation(np.resize(levels, k // 512 * 4)).reshape(k // 512, 4)
    idx = np.arange(k)
    return np.exp2(a[idx // 512, idx % 128 // 32])


BF16 = ml_dtypes.bfloat16


def bf(x):
    return np.asarray(x, np.float32).astype(BF16)


def f64(x):
    return np.asarray(x).astype(np.float64)


E2M1 = np.array([0.0, 0.5, 1.0, 1.5, 2.0, 3.0, 4.0, 6.0, -0.0, -0.5, -1.0, -1.5, -2.0, -3.0, -4.0, -6.0])


def pack_weight(w, fmt):
    k, n = w.shape
    w = f64(bf(w)).reshape(k // 32, 32, n)
    amax = np.abs(w).max(1)
    if fmt == "e4m3":
        byte = np.frexp(amax)[1] - 1 + 127 - 7
    else:
        mant, ex = np.frexp(amax / 6.0)
        byte = np.where(mant > 0.5, ex, ex - 1) + 127
    byte = np.clip(np.where(amax > 0, byte, 1), 1, 254)
    scaled = (w * np.exp2(127.0 - byte)[:, None, :]).reshape(k, n).astype(np.float32)
    by_word = np.ascontiguousarray(scaled.reshape(k // 512, 128, 4, n).transpose(0, 1, 3, 2))
    if fmt == "e4m3":
        words = by_word.astype(ml_dtypes.float8_e4m3fn).view(np.uint8)
    else:
        c = by_word.astype(ml_dtypes.float4_e2m1fn).view(np.uint8) & 0xF
        words = c[..., 0::2] | (c[..., 1::2] << 4)
    return np.ascontiguousarray(words), np.ascontiguousarray(byte.astype(np.uint8).reshape(k // 512, 16, n))


def unpack_weight(words, scales, fmt):
    g, p, n, _ = words.shape
    if fmt == "e4m3":
        vals = np.ascontiguousarray(words).view(ml_dtypes.float8_e4m3fn).astype(np.float64)
    else:
        nib = np.empty((g, p, n, 4), np.uint8)
        nib[..., 0::2] = words & 0xF
        nib[..., 1::2] = words >> 4
        vals = E2M1[nib]
    vals = vals * np.repeat(np.exp2(scales.astype(np.float64) - 127.0), 8, axis=1)[..., None]
    return vals.transpose(0, 1, 3, 2).reshape(g * 512, n)

def pack4(w):
    words, scales = pack_weight(w, "e2m1")
    return words.reshape(words.shape[0], 128, -1), scales


def unpack4(words, scales):
    return unpack_weight(words.reshape(words.shape[0], 128, -1, 2), scales, "e2m1")


B, T, D, H, HD, Q_STRIDE, WINDOW, QKV = 1, 1536, 1024, 16, 64, 4, 128, 3
NW = T // (Q_STRIDE * WINDOW)
SEQ = T // NW


def setup_inputs():
    s = mx_kscale(D)
    embeddings = bf(np.random.standard_normal((B, T, D)) * s)
    qkv_w = np.random.standard_normal((QKV * D, D)) / np.sqrt(D) / s[None, :]
    words, scales = pack4(np.ascontiguousarray(qkv_w.T))
    qkv_b = bf(np.random.standard_normal(QKV * D) * 0.3)
    return {"embeddings": embeddings,
            "qkv_w_words": words,
            "qkv_w_scales": scales,
            "qkv_b": qkv_b}


def reference(embeddings, qkv_w_words, qkv_w_scales, qkv_b):
    y = (mxq(f64(embeddings), 2, "e4m3") @ unpack4(qkv_w_words, qkv_w_scales)) + f64(qkv_b)
    qkv = y.reshape(B, SEQ, NW, QKV, H, HD)
    qkv = qkv.transpose(3, 0, 4, 2, 1, 5)
    q, k, v = qkv[0], qkv[1], qkv[2]
    q = q.reshape(B, H, NW, Q_STRIDE, SEQ // Q_STRIDE, HD).max(axis=3)
    return q, k, v

@@ -1,0 +1,238 @@
+import concourse.mybir as mybir
+from concourse.masks import make_identity
+
+F32 = mybir.dt.float32
+BF16 = mybir.dt.bfloat16
+I32 = mybir.dt.int32
+U32 = mybir.dt.uint32
+U8 = mybir.dt.uint8
+FP8X4 = mybir.dt.float8_e4m3fn_x4
+FP4X4 = mybir.dt.float4_e2m1fn_x4
+ADD = mybir.AluOpType.add
+MAX = mybir.AluOpType.max
+
+P = 128
+TOKENS, K, CHANNELS = 1536, 1024, 3072
+WINDOWS = 3
+TILES = 4
+PASSES = 2
+HEAD = 64
+BANK = 512
+BANK_HEADS = BANK // HEAD
+PART = 1024
+STRIDES = 4
+
+FLOPS = 2 * TOKENS * K * CHANNELS
+
+
+def tile_hieramaskunitattention_pa_kernel(
+    tc, embeddings, qkv_w_words, qkv_w_scales, qkv_b, out_0, out_1, out_2
+):
+    nc = tc.nc
+    with tc.tile_pool(name="keep", bufs=1) as keep, tc.tile_pool(
+        name="grouped_pool", bufs=2
+    ) as grouped_pool, tc.tile_pool(name="kv_pool", bufs=6) as kv_pool, tc.tile_pool(
+        name="q_pool", bufs=2
+    ) as q_pool, tc.psum_pool(name="psum", bufs=8) as psum, tc.manual_schedule():
+        w_scales = keep.tile([P, PASSES, CHANNELS], U8, align_bytes=64)
+        nc.vector.memset(w_scales[:].bitcast(I32), 0)
+        b_rows = keep.tile([P, CHANNELS], BF16)
+        nc.vector.memset(b_rows[:].bitcast(I32), 0)
+        ones = keep.tile([P, P], BF16)
+        nc.vector.memset(ones[:], 1.0)
+        ident = keep.tile([P, P], F32)
+        make_identity(nc, ident[:])
+
+        x_view = embeddings[0].rearrange("(p j w) k -> w j p k", j=TILES, w=WINDOWS)
+        x_sb = [
+            [keep.tile([P, K], BF16, name="x_%d_%d" % (w, j)) for j in range(TILES)]
+            for w in range(WINDOWS)
+        ]
+        words_view = qkv_w_words.bitcast(I32)
+        w_words = [
+            [
+                keep.tile([P, 2 * PART], U8, name="w_words_%d_%d" % (part, g), align_bytes=64)
+                for g in range(PASSES)
+            ]
+            for part in range(3)
+        ]
+
+        def load_x(w):
+            for j in range(TILES):
+                nc.sync.dma_start(out=x_sb[w][j][:], in_=x_view[w, j])
+
+        def load_words(part):
+            cols = slice(part * 2 * PART // 4, (part + 1) * 2 * PART // 4)
+            for g in range(PASSES):
+                nc.sync.dma_start(
+                    out=w_words[part][g][:].bitcast(I32), in_=words_view[g, :, cols]
+                )
+
+        nc.scalar.dma_start(out=b_rows[0:1, :], in_=qkv_b.rearrange("(o n) -> o n", o=1))
+        load_x(0)
+        scales_view = qkv_w_scales.bitcast(I32)
+        planes_view = w_scales[:].bitcast(I32)
+        for half in range(2):
+            for r in range(4):
+                nc.sync.dma_start(
+                    out=planes_view[32 * half + r : P : 64],
+                    in_=scales_view[:, 4 * half + r : 16 : 8, :].rearrange("g q n -> q g n"),
+                )
+        load_words(0)
+        load_words(1)
+        load_x(1)
+        load_words(2)
+        load_x(2)
+
+        bias = keep.tile([P, CHANNELS], F32)
+
+        def spread_bias():
+            for n0 in range(0, CHANNELS, BANK):
+                bias_ps = psum.tile([P, BANK], F32, tag="bank")
+                nc.tensor.matmul(
+                    out=bias_ps[:],
+                    lhsT=ones[:],
+                    rhs=b_rows[:, n0 : n0 + BANK],
+                    start=True,
+                    stop=True,
+                )
+                nc.scalar.copy(out=bias[:, n0 : n0 + BANK], in_=bias_ps[:])
+
+        def by_head(ap):
+            return ap.rearrange("p (h d) -> p h d", d=HEAD)
+
+        x_codes = [
+            keep.tile([P, PASSES, TILES * P], U32, name="x_codes_%d" % w, align_bytes=64)
+            for w in range(WINDOWS)
+        ]
+        x_scales = [
+            keep.tile([P, PASSES, TILES * P], U8, name="x_scales_%d" % w, align_bytes=64)
+            for w in range(WINDOWS)
+        ]
+        grouped = {}
+
+        def transpose_window(w):
+            grouped[w] = grouped_pool.tile(
+                [P, PASSES, TILES, P, 4], BF16, name="grouped", align_bytes=64
+            )
+            for j in range(TILES):
+                x_words = x_sb[w][j][:].bitcast(F32)
+                xt = psum.tile([P, BANK], F32, tag="bank")
+                for g in range(PASSES):
+                    for u in range(2):
+                        a = 2 * g + u
+                        nc.tensor.transpose(
+                            out=xt[:, a * P : (a + 1) * P],
+                            in_=x_words[:, 256 * g + u : 256 * (g + 1) : 2],
+                            identity=ident[:],
+                        )
+                nc.scalar.copy(
+                    out=grouped[w][:].bitcast(F32)[:, :, j],
+                    in_=xt[:].rearrange("p (g u t) -> p g t u", g=PASSES, u=2),
+                )
+
+        def quantise_window(w):
+            for g in range(PASSES):
+                nc.vector.quantize_mx(
+                    out=x_codes[w][:, g, :].bitcast(FP8X4),
+                    scales=x_scales[w][:, g, :],
+                    in_=grouped[w][:, g].rearrange("p j t f -> p (j t f)"),
+                )
+
+        def kv_unit(w, c, vector_only):
+            part = 1 + c // 2
+            local = (c % 2) * BANK
+            n0 = part * PART + local
+            kv_sb = kv_pool.tile([P, BANK_HEADS, TILES, HEAD], F32, name="kv_sb")
+            for j in range(TILES):
+                acc = psum.tile([P, BANK], F32, tag="bank")
+                for g in range(PASSES):
+                    nc.tensor.matmul_mx(
+                        out=acc[:],
+                        lhsT=x_codes[w][:, g, j * P : (j + 1) * P].bitcast(FP8X4),
+                        lhsT_scale=x_scales[w][:, g, j * P : (j + 1) * P],
+                        rhs=w_words[part][g][:, 2 * local : 2 * (local + BANK)].bitcast(FP4X4),
+                        rhs_scale=w_scales[:, g, n0 : n0 + BANK],
+                        start=(g == 0),
+                        stop=(g == PASSES - 1),
+                    )
+                if vector_only or j % 2 == 1:
+                    nc.vector.tensor_tensor(
+                        out=kv_sb[:, :, j, :],
+                        in0=by_head(acc[:]),
+                        in1=by_head(bias[:, n0 : n0 + BANK]),
+                        op=ADD,
+                    )
+                else:
+                    nc.scalar.copy(out=kv_sb[:, :, j, :], in_=by_head(acc[:]))
+                    nc.gpsimd.tensor_tensor(
+                        out=kv_sb[:, :, j, :],
+                        in0=kv_sb[:, :, j, :],
+                        in1=by_head(bias[:, n0 : n0 + BANK]),
+                        op=ADD,
+                    )
+            dest = out_1 if part == 1 else out_2
+            h0 = local // HEAD
+            nc.sync.dma_start(
+                out=dest[0, h0 : h0 + BANK_HEADS, w].rearrange("h (p j) d -> p h (j d)", j=TILES),
+                in_=kv_sb[:].rearrange("p h j d -> p h (j d)"),
+            )
+
+        q_t = {}
+
+        def q_groups(w, first, count):
+            if first == 0:
+                q_t[w] = q_pool.tile([P, PART // P, P], F32, name="q_t")
+            for c in range(first, first + count):
+                acc = psum.tile([P, BANK], F32, tag="bank")
+                for g in range(PASSES):
+                    nc.tensor.matmul_mx(
+                        out=acc[:],
+                        lhsT=w_words[0][g][:, 2 * c * P : 2 * (c + 1) * P].bitcast(FP4X4),
+                        lhsT_scale=w_scales[:, g, c * P : (c + 1) * P],
+                        rhs=x_codes[w][:, g, :].bitcast(FP8X4),
+                        rhs_scale=x_scales[w][:, g, :],
+                        start=(g == 0),
+                        stop=(g == PASSES - 1),
+                    )
+                nc.vector.tensor_reduce(
+                    out=q_t[w][:, c, :].rearrange("c (r j) -> c r j", j=TILES),
+                    in_=acc[:].rearrange("c (j s r) -> c r j s", j=TILES, s=STRIDES),
+                    axis=mybir.AxisListType.X,
+                    op=MAX,
+                )
+
+        def q_finish(w):
+            q_sb = q_pool.tile([P, PART // HEAD, HEAD], F32, name="q_sb")
+            for b in range(PART // BANK):
+                back = psum.tile([P, BANK], F32, tag="bank")
+                for a in range(BANK // P):
+                    nc.tensor.transpose(
+                        out=back[:, a * P : (a + 1) * P],
+                        in_=q_t[w][:, b * (BANK // P) + a, :],
+                        identity=ident[:],
+                    )
+                nc.vector.tensor_tensor(
+                    out=q_sb[:, b * BANK_HEADS : (b + 1) * BANK_HEADS, :],
+                    in0=by_head(back[:]),
+                    in1=by_head(bias[:, b * BANK : (b + 1) * BANK]),
+                    op=ADD,
+                )
+            nc.sync.dma_start(out=out_0[0, :, w].rearrange("h i d -> i h d"), in_=q_sb[:])
+
+        transpose_window(0)
+        quantise_window(0)
+        spread_bias()
+        for w in range(WINDOWS):
+            last = w == WINDOWS - 1
+            q_groups(w, 0, 4)
+            kv_unit(w, 0, False)
+            q_groups(w, 4, 4)
+            kv_unit(w, 1, False)
+            if not last:
+                transpose_window(w + 1)
+            q_finish(w)
+            if not last:
+                quantise_window(w + 1)
+            kv_unit(w, 2, False)
+            kv_unit(w, 3, last)

@@ -20,7 +20,11 @@ HEAD = 64
 BANK = 512
 BANK_HEADS = BANK // HEAD
 PART = 1024
+UNITS = 2 * PART // BANK
 STRIDES = 4
+TWO_STEP_TILE = 1
+PART_ORDER = (1, 2, 0)
+Q_LAG = 2
 
 FLOPS = 2 * TOKENS * K * CHANNELS
 
@@ -32,16 +36,20 @@ def tile_hieramaskunitattention_pa_kernel(
     with tc.tile_pool(name="keep", bufs=1) as keep, tc.tile_pool(
         name="grouped_pool", bufs=2
     ) as grouped_pool, tc.tile_pool(name="kv_pool", bufs=6) as kv_pool, tc.tile_pool(
-        name="q_pool", bufs=2
-    ) as q_pool, tc.psum_pool(name="psum", bufs=8) as psum, tc.manual_schedule():
-        w_scales = keep.tile([P, PASSES, CHANNELS], U8, align_bytes=64)
-        nc.vector.memset(w_scales[:].bitcast(I32), 0)
+        name="fine_pool", bufs=4
+    ) as fine_pool, tc.tile_pool(name="q_pool", bufs=2) as q_pool, tc.psum_pool(
+        name="psum", bufs=8
+    ) as psum, tc.manual_schedule():
         b_rows = keep.tile([P, CHANNELS], BF16)
         nc.vector.memset(b_rows[:].bitcast(I32), 0)
+        w_scales = keep.tile([P, PASSES, CHANNELS], U8, align_bytes=64)
+        nc.vector.memset(w_scales[:].bitcast(I32), 0)
         ones = keep.tile([P, P], BF16)
         nc.vector.memset(ones[:], 1.0)
         ident = keep.tile([P, P], F32)
         make_identity(nc, ident[:])
+        warm = keep.tile([P, 1], BF16)
+        nc.scalar.copy(out=warm[:], in_=ones[:, 0:1])
 
         x_view = embeddings[0].rearrange("(p j w) k -> w j p k", j=TILES, w=WINDOWS)
         x_sb = [
@@ -78,16 +86,16 @@ def tile_hieramaskunitattention_pa_kernel(
                     out=planes_view[32 * half + r : P : 64],
                     in_=scales_view[:, 4 * half + r : 16 : 8, :].rearrange("g q n -> q g n"),
                 )
-        load_words(0)
-        load_words(1)
+        load_words(PART_ORDER[0])
         load_x(1)
-        load_words(2)
+        load_words(PART_ORDER[1])
         load_x(2)
+        load_words(PART_ORDER[2])
 
         bias = keep.tile([P, CHANNELS], F32)
 
-        def spread_bias():
-            for n0 in range(0, CHANNELS, BANK):
+        def spread_bias(part):
+            for n0 in range(part * PART, (part + 1) * PART, BANK):
                 bias_ps = psum.tile([P, BANK], F32, tag="bank")
                 nc.tensor.matmul(
                     out=bias_ps[:],
@@ -110,60 +118,73 @@ def tile_hieramaskunitattention_pa_kernel(
             for w in range(WINDOWS)
         ]
         grouped = {}
+        x_sorted = [
+            [keep.tile([P, K // 2], F32, name="x_sorted_%d_%d" % (w, j)) for j in range(TILES)]
+            for w in range(WINDOWS)
+        ]
 
-        def transpose_window(w):
-            grouped[w] = grouped_pool.tile(
-                [P, PASSES, TILES, P, 4], BF16, name="grouped", align_bytes=64
+        def sort_words(w, j):
+            copy = nc.vector.tensor_copy if w == 0 else nc.scalar.copy
+            copy(
+                out=x_sorted[w][j][:].rearrange("t (g u p) -> t g u p", g=PASSES, u=2),
+                in_=x_sb[w][j][:].bitcast(F32).rearrange("t (g p u) -> t g u p", g=PASSES, u=2),
             )
-            for j in range(TILES):
-                x_words = x_sb[w][j][:].bitcast(F32)
-                xt = psum.tile([P, BANK], F32, tag="bank")
-                for g in range(PASSES):
-                    for u in range(2):
-                        a = 2 * g + u
-                        nc.tensor.transpose(
-                            out=xt[:, a * P : (a + 1) * P],
-                            in_=x_words[:, 256 * g + u : 256 * (g + 1) : 2],
-                            identity=ident[:],
-                        )
-                nc.scalar.copy(
-                    out=grouped[w][:].bitcast(F32)[:, :, j],
-                    in_=xt[:].rearrange("p (g u t) -> p g t u", g=PASSES, u=2),
-                )
 
-        def quantise_window(w):
+        def transpose_tile(w, j):
+            if j == 0:
+                grouped[w] = grouped_pool.tile(
+                    [P, TILES, PASSES, P, 4], BF16, name="grouped", align_bytes=64
+                )
+            xt = psum.tile([P, BANK], F32, tag="bank")
+            for a in range(BANK // P):
+                nc.tensor.transpose(
+                    out=xt[:, a * P : (a + 1) * P],
+                    in_=x_sorted[w][j][:, a * P : (a + 1) * P],
+                    identity=ident[:],
+                )
+            nc.scalar.copy(
+                out=grouped[w][:].bitcast(F32)[:, j],
+                in_=xt[:].rearrange("p (g u t) -> p g t u", g=PASSES, u=2),
+            )
+
+        def quantise_tile(w, j):
             for g in range(PASSES):
                 nc.vector.quantize_mx(
-                    out=x_codes[w][:, g, :].bitcast(FP8X4),
-                    scales=x_scales[w][:, g, :],
-                    in_=grouped[w][:, g].rearrange("p j t f -> p (j t f)"),
+                    out=x_codes[w][:, g, j * P : (j + 1) * P].bitcast(FP8X4),
+                    scales=x_scales[w][:, g, j * P : (j + 1) * P],
+                    in_=grouped[w][:, j, g].rearrange("p t f -> p (t f)"),
                 )
 
-        def kv_unit(w, c, vector_only):
+        def kv_products(acc, w, j, part, local, width):
+            n0 = part * PART + local
+            for g in range(PASSES):
+                nc.tensor.matmul_mx(
+                    out=acc,
+                    lhsT=x_codes[w][:, g, j * P : (j + 1) * P].bitcast(FP8X4),
+                    lhsT_scale=x_scales[w][:, g, j * P : (j + 1) * P],
+                    rhs=w_words[part][g][:, 2 * local : 2 * (local + width)].bitcast(FP4X4),
+                    rhs_scale=w_scales[:, g, n0 : n0 + width],
+                    start=(g == 0),
+                    stop=(g == PASSES - 1),
+                )
+
+        def kv_store(w, part, local, heads, tile_sb):
+            dest = out_1 if part == 1 else out_2
+            h0 = local // HEAD
+            nc.sync.dma_start(
+                out=dest[0, h0 : h0 + heads, w].rearrange("h (p j) d -> p h (j d)", j=TILES),
+                in_=tile_sb.rearrange("p h j d -> p h (j d)"),
+            )
+
+        def kv_unit(w, c):
             part = 1 + c // 2
             local = (c % 2) * BANK
             n0 = part * PART + local
             kv_sb = kv_pool.tile([P, BANK_HEADS, TILES, HEAD], F32, name="kv_sb")
             for j in range(TILES):
                 acc = psum.tile([P, BANK], F32, tag="bank")
-                for g in range(PASSES):
-                    nc.tensor.matmul_mx(
-                        out=acc[:],
-                        lhsT=x_codes[w][:, g, j * P : (j + 1) * P].bitcast(FP8X4),
-                        lhsT_scale=x_scales[w][:, g, j * P : (j + 1) * P],
-                        rhs=w_words[part][g][:, 2 * local : 2 * (local + BANK)].bitcast(FP4X4),
-                        rhs_scale=w_scales[:, g, n0 : n0 + BANK],
-                        start=(g == 0),
-                        stop=(g == PASSES - 1),
-                    )
-                if vector_only or j % 2 == 1:
-                    nc.vector.tensor_tensor(
-                        out=kv_sb[:, :, j, :],
-                        in0=by_head(acc[:]),
-                        in1=by_head(bias[:, n0 : n0 + BANK]),
-                        op=ADD,
-                    )
-                else:
+                kv_products(acc[:], w, j, part, local, BANK)
+                if j == TWO_STEP_TILE:
                     nc.scalar.copy(out=kv_sb[:, :, j, :], in_=by_head(acc[:]))
                     nc.gpsimd.tensor_tensor(
                         out=kv_sb[:, :, j, :],
@@ -171,40 +192,64 @@ def tile_hieramaskunitattention_pa_kernel(
                         in1=by_head(bias[:, n0 : n0 + BANK]),
                         op=ADD,
                     )
-            dest = out_1 if part == 1 else out_2
-            h0 = local // HEAD
-            nc.sync.dma_start(
-                out=dest[0, h0 : h0 + BANK_HEADS, w].rearrange("h (p j) d -> p h (j d)", j=TILES),
-                in_=kv_sb[:].rearrange("p h j d -> p h (j d)"),
+                else:
+                    nc.vector.tensor_tensor(
+                        out=kv_sb[:, :, j, :],
+                        in0=by_head(acc[:]),
+                        in1=by_head(bias[:, n0 : n0 + BANK]),
+                        op=ADD,
+                    )
+            kv_store(w, part, local, BANK_HEADS, kv_sb[:])
+
+        def kv_fine(w, c, sub):
+            part = 1 + c // 2
+            local = (c % 2) * BANK + sub * P
+            n0 = part * PART + local
+            heads = P // HEAD
+            fine_sb = fine_pool.tile([P, heads, TILES, HEAD], F32, name="fine_sb")
+            acc = psum.tile([P, BANK], F32, tag="bank")
+            for j in range(TILES):
+                kv_products(acc[:, j * P : (j + 1) * P], w, j, part, local, P)
+            nc.vector.tensor_tensor(
+                out=fine_sb[:],
+                in0=acc[:].rearrange("p (j h d) -> p h j d", j=TILES, d=HEAD),
+                in1=by_head(bias[:, n0 : n0 + P])
+                .unsqueeze(2)
+                .to_broadcast([P, heads, TILES, HEAD]),
+                op=ADD,
             )
+            kv_store(w, part, local, heads, fine_sb[:])
 
         q_t = {}
 
-        def q_groups(w, first, count):
-            if first == 0:
-                q_t[w] = q_pool.tile([P, PART // P, P], F32, name="q_t")
-            for c in range(first, first + count):
-                acc = psum.tile([P, BANK], F32, tag="bank")
-                for g in range(PASSES):
-                    nc.tensor.matmul_mx(
-                        out=acc[:],
-                        lhsT=w_words[0][g][:, 2 * c * P : 2 * (c + 1) * P].bitcast(FP4X4),
-                        lhsT_scale=w_scales[:, g, c * P : (c + 1) * P],
-                        rhs=x_codes[w][:, g, :].bitcast(FP8X4),
-                        rhs_scale=x_scales[w][:, g, :],
-                        start=(g == 0),
-                        stop=(g == PASSES - 1),
-                    )
-                nc.vector.tensor_reduce(
-                    out=q_t[w][:, c, :].rearrange("c (r j) -> c r j", j=TILES),
-                    in_=acc[:].rearrange("c (j s r) -> c r j s", j=TILES, s=STRIDES),
-                    axis=mybir.AxisListType.X,
-                    op=MAX,
-                )
+        q_sb = {}
 
-        def q_finish(w):
-            q_sb = q_pool.tile([P, PART // HEAD, HEAD], F32, name="q_sb")
+        def q_group(w, c):
+            if c == 0:
+                q_t[w] = q_pool.tile([P, PART // P, P], F32, name="q_t")
+            acc = psum.tile([P, BANK], F32, tag="bank")
+            for g in range(PASSES):
+                nc.tensor.matmul_mx(
+                    out=acc[:],
+                    lhsT=w_words[0][g][:, 2 * c * P : 2 * (c + 1) * P].bitcast(FP4X4),
+                    lhsT_scale=w_scales[:, g, c * P : (c + 1) * P],
+                    rhs=x_codes[w][:, g, :].bitcast(FP8X4),
+                    rhs_scale=x_scales[w][:, g, :],
+                    start=(g == 0),
+                    stop=(g == PASSES - 1),
+                )
+            nc.vector.tensor_reduce(
+                out=q_t[w][:, c, :].rearrange("c (r j) -> c r j", j=TILES),
+                in_=acc[:].rearrange("c (j s r) -> c r j s", j=TILES, s=STRIDES),
+                axis=mybir.AxisListType.X,
+                op=MAX,
+            )
+
+        def q_back(w):
+            q_sb[w] = q_pool.tile([P, PART // HEAD, HEAD], F32, name="q_sb")
             for b in range(PART // BANK):
+                heads = slice(b * BANK_HEADS, (b + 1) * BANK_HEADS)
+                bias_b = by_head(bias[:, b * BANK : (b + 1) * BANK])
                 back = psum.tile([P, BANK], F32, tag="bank")
                 for a in range(BANK // P):
                     nc.tensor.transpose(
@@ -212,27 +257,50 @@ def tile_hieramaskunitattention_pa_kernel(
                         in_=q_t[w][:, b * (BANK // P) + a, :],
                         identity=ident[:],
                     )
-                nc.vector.tensor_tensor(
-                    out=q_sb[:, b * BANK_HEADS : (b + 1) * BANK_HEADS, :],
-                    in0=by_head(back[:]),
-                    in1=by_head(bias[:, b * BANK : (b + 1) * BANK]),
-                    op=ADD,
-                )
-            nc.sync.dma_start(out=out_0[0, :, w].rearrange("h i d -> i h d"), in_=q_sb[:])
+                if b == 0:
+                    nc.scalar.copy(out=q_sb[w][:, heads, :], in_=by_head(back[:]))
+                    nc.gpsimd.tensor_tensor(
+                        out=q_sb[w][:, heads, :], in0=q_sb[w][:, heads, :], in1=bias_b, op=ADD
+                    )
+                else:
+                    nc.vector.tensor_tensor(
+                        out=q_sb[w][:, heads, :], in0=by_head(back[:]), in1=bias_b, op=ADD
+                    )
 
-        transpose_window(0)
-        quantise_window(0)
-        spread_bias()
+        def q_store(w):
+            nc.sync.dma_start(out=out_0[0, :, w].rearrange("h i d -> i h d"), in_=q_sb[w][:])
+
+        for j in range(TILES):
+            sort_words(0, j)
+        for j in range(TILES):
+            transpose_tile(0, j)
+            quantise_tile(0, j)
+        spread_bias(PART_ORDER[0])
         for w in range(WINDOWS):
             last = w == WINDOWS - 1
-            q_groups(w, 0, 4)
-            kv_unit(w, 0, False)
-            q_groups(w, 4, 4)
-            kv_unit(w, 1, False)
+            kv_unit(w, 0)
             if not last:
-                transpose_window(w + 1)
-            q_finish(w)
+                for j in range(TILES):
+                    sort_words(w + 1, j)
+            kv_unit(w, 1)
             if not last:
-                quantise_window(w + 1)
-            kv_unit(w, 2, False)
-            kv_unit(w, 3, last)
+                for j in range(TILES):
+                    transpose_tile(w + 1, j)
+                spread_bias(PART_ORDER[w + 1])
+            kv_unit(w, 2)
+            if not last:
+                for j in range(TILES):
+                    quantise_tile(w + 1, j)
+                kv_unit(w, 3)
+        for w in range(WINDOWS):
+            for c in range(PART // P):
+                q_group(w, c)
+                if w > 0 and c == Q_LAG - 1:
+                    q_back(w - 1)
+                    q_store(w - 1)
+        kv_fine(WINDOWS - 1, UNITS - 1, 0)
+        q_back(WINDOWS - 1)
+        kv_fine(WINDOWS - 1, UNITS - 1, 1)
+        q_store(WINDOWS - 1)
+        kv_fine(WINDOWS - 1, UNITS - 1, 2)
+        kv_fine(WINDOWS - 1, UNITS - 1, 3)

@@ -58,10 +58,7 @@ def tile_hieramaskunitattention_pa_kernel(
         ]
         words_view = qkv_w_words.bitcast(I32)
         w_words = [
-            [
-                keep.tile([P, 2 * PART], U8, name="w_words_%d_%d" % (part, g), align_bytes=64)
-                for g in range(PASSES)
-            ]
+            keep.tile([P, PASSES, 2 * PART], U8, name="w_words_%d" % part, align_bytes=64)
             for part in range(3)
         ]
 
@@ -69,28 +66,36 @@ def tile_hieramaskunitattention_pa_kernel(
             for j in range(TILES):
                 nc.sync.dma_start(out=x_sb[w][j][:], in_=x_view[w, j])
 
-        def load_words(part):
-            cols = slice(part * 2 * PART // 4, (part + 1) * 2 * PART // 4)
-            for g in range(PASSES):
-                nc.sync.dma_start(
-                    out=w_words[part][g][:].bitcast(I32), in_=words_view[g, :, cols]
-                )
+        def load_words(part, first, width):
+            nc.sync.dma_start(
+                out=w_words[part][:].bitcast(I32)[:, :, first // 2 : (first + width) // 2],
+                in_=words_view[
+                    :, :, (part * PART + first) // 2 : (part * PART + first + width) // 2
+                ].rearrange("g p n -> p g n"),
+            )
 
-        nc.scalar.dma_start(out=b_rows[0:1, :], in_=qkv_b.rearrange("(o n) -> o n", o=1))
-        load_x(0)
         scales_view = qkv_w_scales.bitcast(I32)
         planes_view = w_scales[:].bitcast(I32)
-        for half in range(2):
+
+        def load_scales(part):
+            cols = slice(part * PART // 4, (part + 1) * PART // 4)
             for r in range(4):
                 nc.sync.dma_start(
-                    out=planes_view[32 * half + r : P : 64],
-                    in_=scales_view[:, 4 * half + r : 16 : 8, :].rearrange("g q n -> q g n"),
+                    out=planes_view[r:P:32, :, cols],
+                    in_=scales_view[:, r:16:4, cols].rearrange("g q n -> q g n"),
                 )
-        load_words(PART_ORDER[0])
+
+        load_x(0)
+        nc.scalar.dma_start(out=b_rows[0:1, :], in_=qkv_b.rearrange("(o n) -> o n", o=1))
+        load_words(PART_ORDER[0], 0, BANK)
+        load_scales(PART_ORDER[0])
+        load_words(PART_ORDER[0], BANK, BANK)
         load_x(1)
-        load_words(PART_ORDER[1])
+        load_scales(PART_ORDER[1])
+        load_words(PART_ORDER[1], 0, PART)
         load_x(2)
-        load_words(PART_ORDER[2])
+        load_scales(PART_ORDER[2])
+        load_words(PART_ORDER[2], 0, PART)
 
         bias = keep.tile([P, CHANNELS], F32)
 
@@ -162,7 +167,7 @@ def tile_hieramaskunitattention_pa_kernel(
                     out=acc,
                     lhsT=x_codes[w][:, g, j * P : (j + 1) * P].bitcast(FP8X4),
                     lhsT_scale=x_scales[w][:, g, j * P : (j + 1) * P],
-                    rhs=w_words[part][g][:, 2 * local : 2 * (local + width)].bitcast(FP4X4),
+                    rhs=w_words[part][:, g, 2 * local : 2 * (local + width)].bitcast(FP4X4),
                     rhs_scale=w_scales[:, g, n0 : n0 + width],
                     start=(g == 0),
                     stop=(g == PASSES - 1),
@@ -231,7 +236,7 @@ def tile_hieramaskunitattention_pa_kernel(
             for g in range(PASSES):
                 nc.tensor.matmul_mx(
                     out=acc[:],
-                    lhsT=w_words[0][g][:, 2 * c * P : 2 * (c + 1) * P].bitcast(FP4X4),
+                    lhsT=w_words[0][:, g, 2 * c * P : 2 * (c + 1) * P].bitcast(FP4X4),
                     lhsT_scale=w_scales[:, g, c * P : (c + 1) * P],
                     rhs=x_codes[w][:, g, :].bitcast(FP8X4),
                     rhs_scale=x_scales[w][:, g, :],

@@ -42,8 +42,12 @@ def tile_hieramaskunitattention_pa_kernel(
     ) as psum, tc.manual_schedule():
         b_rows = keep.tile([P, CHANNELS], BF16)
         nc.vector.memset(b_rows[:].bitcast(I32), 0)
-        w_scales = keep.tile([P, PASSES, CHANNELS], U8, align_bytes=64)
-        nc.vector.memset(w_scales[:].bitcast(I32), 0)
+        w_scales = [
+            keep.tile([P, PASSES, PART], U8, name="w_scales_%d" % part, align_bytes=64)
+            for part in range(3)
+        ]
+        for part in PART_ORDER:
+            nc.vector.memset(w_scales[part][:].bitcast(I32), 0)
         ones = keep.tile([P, P], BF16)
         nc.vector.memset(ones[:], 1.0)
         ident = keep.tile([P, P], F32)
@@ -58,7 +62,12 @@ def tile_hieramaskunitattention_pa_kernel(
         ]
         words_view = qkv_w_words.bitcast(I32)
         w_words = [
-            keep.tile([P, PASSES, 2 * PART], U8, name="w_words_%d" % part, align_bytes=64)
+            [
+                keep.tile(
+                    [P, PASSES, 2 * BANK], U8, name="w_words_%d_%d" % (part, b), align_bytes=64
+                )
+                for b in range(PART // BANK)
+            ]
             for part in range(3)
         ]
 
@@ -66,36 +75,36 @@ def tile_hieramaskunitattention_pa_kernel(
             for j in range(TILES):
                 nc.sync.dma_start(out=x_sb[w][j][:], in_=x_view[w, j])
 
-        def load_words(part, first, width):
+        def load_words(part, b):
+            first = (part * PART + b * BANK) // 2
             nc.sync.dma_start(
-                out=w_words[part][:].bitcast(I32)[:, :, first // 2 : (first + width) // 2],
-                in_=words_view[
-                    :, :, (part * PART + first) // 2 : (part * PART + first + width) // 2
-                ].rearrange("g p n -> p g n"),
+                out=w_words[part][b][:].bitcast(I32),
+                in_=words_view[:, :, first : first + BANK // 2].rearrange("g p n -> p g n"),
             )
 
         scales_view = qkv_w_scales.bitcast(I32)
-        planes_view = w_scales[:].bitcast(I32)
 
         def load_scales(part):
             cols = slice(part * PART // 4, (part + 1) * PART // 4)
             for r in range(4):
                 nc.sync.dma_start(
-                    out=planes_view[r:P:32, :, cols],
+                    out=w_scales[part][:].bitcast(I32)[r:P:32],
                     in_=scales_view[:, r:16:4, cols].rearrange("g q n -> q g n"),
                 )
 
         load_x(0)
         nc.scalar.dma_start(out=b_rows[0:1, :], in_=qkv_b.rearrange("(o n) -> o n", o=1))
-        load_words(PART_ORDER[0], 0, BANK)
+        load_words(PART_ORDER[0], 0)
         load_scales(PART_ORDER[0])
-        load_words(PART_ORDER[0], BANK, BANK)
+        load_words(PART_ORDER[0], 1)
         load_x(1)
         load_scales(PART_ORDER[1])
-        load_words(PART_ORDER[1], 0, PART)
+        load_words(PART_ORDER[1], 0)
+        load_words(PART_ORDER[1], 1)
         load_x(2)
         load_scales(PART_ORDER[2])
-        load_words(PART_ORDER[2], 0, PART)
+        load_words(PART_ORDER[2], 0)
+        load_words(PART_ORDER[2], 1)
 
         bias = keep.tile([P, CHANNELS], F32)
 
@@ -167,8 +176,10 @@ def tile_hieramaskunitattention_pa_kernel(
                     out=acc,
                     lhsT=x_codes[w][:, g, j * P : (j + 1) * P].bitcast(FP8X4),
                     lhsT_scale=x_scales[w][:, g, j * P : (j + 1) * P],
-                    rhs=w_words[part][:, g, 2 * local : 2 * (local + width)].bitcast(FP4X4),
-                    rhs_scale=w_scales[:, g, n0 : n0 + width],
+                    rhs=w_words[part][local // BANK][
+                        :, g, 2 * (local % BANK) : 2 * (local % BANK + width)
+                    ].bitcast(FP4X4),
+                    rhs_scale=w_scales[part][:, g, local : local + width],
                     start=(g == 0),
                     stop=(g == PASSES - 1),
                 )
@@ -236,8 +247,10 @@ def tile_hieramaskunitattention_pa_kernel(
             for g in range(PASSES):
                 nc.tensor.matmul_mx(
                     out=acc[:],
-                    lhsT=w_words[0][:, g, 2 * c * P : 2 * (c + 1) * P].bitcast(FP4X4),
-                    lhsT_scale=w_scales[:, g, c * P : (c + 1) * P],
+                    lhsT=w_words[0][c * P // BANK][
+                        :, g, 2 * (c * P % BANK) : 2 * (c * P % BANK + P)
+                    ].bitcast(FP4X4),
+                    lhsT_scale=w_scales[0][:, g, c * P : (c + 1) * P],
                     rhs=x_codes[w][:, g, :].bitcast(FP8X4),
                     rhs_scale=x_scales[w][:, g, :],
                     start=(g == 0),

@@ -263,30 +263,33 @@ def tile_hieramaskunitattention_pa_kernel(
                 op=MAX,
             )
 
-        def q_back(w):
-            q_sb[w] = q_pool.tile([P, PART // HEAD, HEAD], F32, name="q_sb")
-            for b in range(PART // BANK):
-                heads = slice(b * BANK_HEADS, (b + 1) * BANK_HEADS)
-                bias_b = by_head(bias[:, b * BANK : (b + 1) * BANK])
-                back = psum.tile([P, BANK], F32, tag="bank")
-                for a in range(BANK // P):
-                    nc.tensor.transpose(
-                        out=back[:, a * P : (a + 1) * P],
-                        in_=q_t[w][:, b * (BANK // P) + a, :],
-                        identity=ident[:],
-                    )
-                if b == 0:
-                    nc.scalar.copy(out=q_sb[w][:, heads, :], in_=by_head(back[:]))
-                    nc.gpsimd.tensor_tensor(
-                        out=q_sb[w][:, heads, :], in0=q_sb[w][:, heads, :], in1=bias_b, op=ADD
-                    )
-                else:
-                    nc.vector.tensor_tensor(
-                        out=q_sb[w][:, heads, :], in0=by_head(back[:]), in1=bias_b, op=ADD
-                    )
+        def q_back(w, b):
+            if b == 0:
+                q_sb[w] = q_pool.tile([P, PART // HEAD, HEAD], F32, name="q_sb")
+            heads = slice(b * BANK_HEADS, (b + 1) * BANK_HEADS)
+            bias_b = by_head(bias[:, b * BANK : (b + 1) * BANK])
+            back = psum.tile([P, BANK], F32, tag="bank")
+            for a in range(BANK // P):
+                nc.tensor.transpose(
+                    out=back[:, a * P : (a + 1) * P],
+                    in_=q_t[w][:, b * (BANK // P) + a, :],
+                    identity=ident[:],
+                )
+            if b == 0:
+                nc.scalar.copy(out=q_sb[w][:, heads, :], in_=by_head(back[:]))
+                nc.gpsimd.tensor_tensor(
+                    out=q_sb[w][:, heads, :], in0=q_sb[w][:, heads, :], in1=bias_b, op=ADD
+                )
+            else:
+                nc.vector.tensor_tensor(
+                    out=q_sb[w][:, heads, :], in0=by_head(back[:]), in1=bias_b, op=ADD
+                )
 
-        def q_store(w):
-            nc.sync.dma_start(out=out_0[0, :, w].rearrange("h i d -> i h d"), in_=q_sb[w][:])
+        def q_store(w, h0, heads):
+            nc.sync.dma_start(
+                out=out_0[0, h0 : h0 + heads, w].rearrange("h i d -> i h d"),
+                in_=q_sb[w][:, h0 : h0 + heads, :],
+            )
 
         for j in range(TILES):
             sort_words(0, j)
@@ -310,15 +313,20 @@ def tile_hieramaskunitattention_pa_kernel(
                 for j in range(TILES):
                     quantise_tile(w + 1, j)
                 kv_unit(w, 3)
+        last_w = WINDOWS - 1
+        fine_after = {(1, 3): 0, (1, 6): 1, (last_w, 3): 2}
         for w in range(WINDOWS):
             for c in range(PART // P):
                 q_group(w, c)
                 if w > 0 and c == Q_LAG - 1:
-                    q_back(w - 1)
-                    q_store(w - 1)
-        kv_fine(WINDOWS - 1, UNITS - 1, 0)
-        q_back(WINDOWS - 1)
-        kv_fine(WINDOWS - 1, UNITS - 1, 1)
-        q_store(WINDOWS - 1)
-        kv_fine(WINDOWS - 1, UNITS - 1, 2)
-        kv_fine(WINDOWS - 1, UNITS - 1, 3)
+                    q_back(w - 1, 0)
+                    q_back(w - 1, 1)
+                    q_store(w - 1, 0, PART // HEAD)
+                if (w, c) in fine_after:
+                    kv_fine(last_w, UNITS - 1, fine_after[(w, c)])
+                if w == last_w and c == BANK // P + Q_LAG - 1:
+                    q_back(w, 0)
+                    q_store(w, 0, BANK_HEADS)
+        kv_fine(last_w, UNITS - 1, 3)
+        q_back(last_w, 1)
+        q_store(last_w, BANK_HEADS, BANK_HEADS)

@@ -24,6 +24,7 @@ UNITS = 2 * PART // BANK
 STRIDES = 4
 TWO_STEP_TILE = 1
 PART_ORDER = (1, 2, 0)
+WARM_UP = 4
 Q_LAG = 2
 
 FLOPS = 2 * TOKENS * K * CHANNELS
@@ -40,18 +41,21 @@ def tile_hieramaskunitattention_pa_kernel(
     ) as fine_pool, tc.tile_pool(name="q_pool", bufs=2) as q_pool, tc.psum_pool(
         name="psum", bufs=8
     ) as psum, tc.manual_schedule():
-        b_rows = keep.tile([P, CHANNELS], BF16)
-        nc.vector.memset(b_rows[:].bitcast(I32), 0)
+        ones = keep.tile([P, BANK], BF16)
+        nc.vector.memset(ones[:], 1.0)
+        b_rows = [keep.tile([P, PART], BF16, name="b_rows_%d" % part) for part in range(3)]
         w_scales = [
             keep.tile([P, PASSES, PART], U8, name="w_scales_%d" % part, align_bytes=64)
             for part in range(3)
         ]
-        for part in PART_ORDER:
-            nc.vector.memset(w_scales[part][:].bitcast(I32), 0)
-        ones = keep.tile([P, P], BF16)
-        nc.vector.memset(ones[:], 1.0)
+        first_part = PART_ORDER[0]
+        nc.vector.memset(b_rows[first_part][:].bitcast(I32), 0)
+        nc.vector.memset(w_scales[first_part][:].bitcast(I32), 0)
         ident = keep.tile([P, P], F32)
         make_identity(nc, ident[:])
+        for part in PART_ORDER[1:]:
+            nc.gpsimd.memset(w_scales[part][:].bitcast(F32), 0.0)
+            nc.gpsimd.memset(b_rows[part][:].bitcast(F32), 0.0)
         warm = keep.tile([P, 1], BF16)
         nc.scalar.copy(out=warm[:], in_=ones[:, 0:1])
 
@@ -92,17 +96,25 @@ def tile_hieramaskunitattention_pa_kernel(
                     in_=scales_view[:, r:16:4, cols].rearrange("g q n -> q g n"),
                 )
 
+        def load_bias(part):
+            nc.sync.dma_start(
+                out=b_rows[part][0:1, :],
+                in_=qkv_b[part * PART : (part + 1) * PART].rearrange("(o n) -> o n", o=1),
+            )
+
         load_x(0)
-        nc.scalar.dma_start(out=b_rows[0:1, :], in_=qkv_b.rearrange("(o n) -> o n", o=1))
+        load_bias(PART_ORDER[0])
         load_words(PART_ORDER[0], 0)
         load_scales(PART_ORDER[0])
         load_words(PART_ORDER[0], 1)
         load_x(1)
         load_scales(PART_ORDER[1])
+        load_bias(PART_ORDER[1])
         load_words(PART_ORDER[1], 0)
         load_words(PART_ORDER[1], 1)
         load_x(2)
         load_scales(PART_ORDER[2])
+        load_bias(PART_ORDER[2])
         load_words(PART_ORDER[2], 0)
         load_words(PART_ORDER[2], 1)
 
@@ -113,12 +125,19 @@ def tile_hieramaskunitattention_pa_kernel(
                 bias_ps = psum.tile([P, BANK], F32, tag="bank")
                 nc.tensor.matmul(
                     out=bias_ps[:],
-                    lhsT=ones[:],
-                    rhs=b_rows[:, n0 : n0 + BANK],
+                    lhsT=ones[:, 0:P],
+                    rhs=b_rows[part][:, n0 - part * PART : n0 - part * PART + BANK],
                     start=True,
                     stop=True,
                 )
                 nc.scalar.copy(out=bias[:, n0 : n0 + BANK], in_=bias_ps[:])
+
+        def warm_up():
+            busy = psum.tile([P, BANK], F32, tag="bank")
+            for r in range(WARM_UP):
+                nc.tensor.matmul(
+                    out=busy[:], lhsT=ones[:, 0:P], rhs=ones[:], start=True, stop=True
+                )
 
         def by_head(ap):
             return ap.rearrange("p (h d) -> p h d", d=HEAD)
@@ -291,6 +310,7 @@ def tile_hieramaskunitattention_pa_kernel(
                 in_=q_sb[w][:, h0 : h0 + heads, :],
             )
 
+        warm_up()
         for j in range(TILES):
             sort_words(0, j)
         for j in range(TILES):

@@ -24,7 +24,7 @@ UNITS = 2 * PART // BANK
 STRIDES = 4
 TWO_STEP_TILE = 1
 PART_ORDER = (1, 2, 0)
-WARM_UP = 4
+WARM_UP = (4, 1, 1, 0)
 Q_LAG = 2
 
 FLOPS = 2 * TOKENS * K * CHANNELS
@@ -49,13 +49,14 @@ def tile_hieramaskunitattention_pa_kernel(
             for part in range(3)
         ]
         first_part = PART_ORDER[0]
-        nc.vector.memset(b_rows[first_part][:].bitcast(I32), 0)
-        nc.vector.memset(w_scales[first_part][:].bitcast(I32), 0)
+
+        def zero(part):
+            nc.vector.memset(b_rows[part][:].bitcast(I32), 0)
+            nc.vector.memset(w_scales[part][:].bitcast(I32), 0)
+
+        zero(first_part)
         ident = keep.tile([P, P], F32)
         make_identity(nc, ident[:])
-        for part in PART_ORDER[1:]:
-            nc.gpsimd.memset(w_scales[part][:].bitcast(F32), 0.0)
-            nc.gpsimd.memset(b_rows[part][:].bitcast(F32), 0.0)
         warm = keep.tile([P, 1], BF16)
         nc.scalar.copy(out=warm[:], in_=ones[:, 0:1])
 
@@ -108,15 +109,12 @@ def tile_hieramaskunitattention_pa_kernel(
         load_scales(PART_ORDER[0])
         load_words(PART_ORDER[0], 1)
         load_x(1)
-        load_scales(PART_ORDER[1])
-        load_bias(PART_ORDER[1])
-        load_words(PART_ORDER[1], 0)
-        load_words(PART_ORDER[1], 1)
-        load_x(2)
-        load_scales(PART_ORDER[2])
-        load_bias(PART_ORDER[2])
-        load_words(PART_ORDER[2], 0)
-        load_words(PART_ORDER[2], 1)
+
+        def load_part(part):
+            load_scales(part)
+            load_bias(part)
+            load_words(part, 0)
+            load_words(part, 1)
 
         bias = keep.tile([P, CHANNELS], F32)
 
@@ -132,9 +130,9 @@ def tile_hieramaskunitattention_pa_kernel(
                 )
                 nc.scalar.copy(out=bias[:, n0 : n0 + BANK], in_=bias_ps[:])
 
-        def warm_up():
+        def warm_up(count):
             busy = psum.tile([P, BANK], F32, tag="bank")
-            for r in range(WARM_UP):
+            for r in range(count):
                 nc.tensor.matmul(
                     out=busy[:], lhsT=ones[:, 0:P], rhs=ones[:], start=True, stop=True
                 )
@@ -282,27 +280,24 @@ def tile_hieramaskunitattention_pa_kernel(
                 op=MAX,
             )
 
-        def q_back(w, b):
-            if b == 0:
+        def q_back(w, first, count):
+            if first == 0:
                 q_sb[w] = q_pool.tile([P, PART // HEAD, HEAD], F32, name="q_sb")
-            heads = slice(b * BANK_HEADS, (b + 1) * BANK_HEADS)
-            bias_b = by_head(bias[:, b * BANK : (b + 1) * BANK])
+            dest = q_sb[w][:, first * P // HEAD : (first + count) * P // HEAD, :]
+            bias_b = by_head(bias[:, first * P : (first + count) * P])
             back = psum.tile([P, BANK], F32, tag="bank")
-            for a in range(BANK // P):
+            for a in range(count):
                 nc.tensor.transpose(
                     out=back[:, a * P : (a + 1) * P],
-                    in_=q_t[w][:, b * (BANK // P) + a, :],
+                    in_=q_t[w][:, first + a, :],
                     identity=ident[:],
                 )
-            if b == 0:
-                nc.scalar.copy(out=q_sb[w][:, heads, :], in_=by_head(back[:]))
-                nc.gpsimd.tensor_tensor(
-                    out=q_sb[w][:, heads, :], in0=q_sb[w][:, heads, :], in1=bias_b, op=ADD
-                )
+            source = by_head(back[:, 0 : count * P])
+            if first == 0 and w < WINDOWS - 1:
+                nc.scalar.copy(out=dest, in_=source)
+                nc.gpsimd.tensor_tensor(out=dest, in0=dest, in1=bias_b, op=ADD)
             else:
-                nc.vector.tensor_tensor(
-                    out=q_sb[w][:, heads, :], in0=by_head(back[:]), in1=bias_b, op=ADD
-                )
+                nc.vector.tensor_tensor(out=dest, in0=source, in1=bias_b, op=ADD)
 
         def q_store(w, h0, heads):
             nc.sync.dma_start(
@@ -310,13 +305,16 @@ def tile_hieramaskunitattention_pa_kernel(
                 in_=q_sb[w][:, h0 : h0 + heads, :],
             )
 
-        warm_up()
         for j in range(TILES):
             sort_words(0, j)
         for j in range(TILES):
+            warm_up(WARM_UP[j])
             transpose_tile(0, j)
             quantise_tile(0, j)
         spread_bias(PART_ORDER[0])
+        zero(PART_ORDER[1])
+        load_part(PART_ORDER[1])
+        load_x(2)
         for w in range(WINDOWS):
             last = w == WINDOWS - 1
             kv_unit(w, 0)
@@ -328,25 +326,31 @@ def tile_hieramaskunitattention_pa_kernel(
                 for j in range(TILES):
                     transpose_tile(w + 1, j)
                 spread_bias(PART_ORDER[w + 1])
+            if w == 0:
+                zero(PART_ORDER[2])
+                load_part(PART_ORDER[2])
             kv_unit(w, 2)
             if not last:
                 for j in range(TILES):
                     quantise_tile(w + 1, j)
                 kv_unit(w, 3)
         last_w = WINDOWS - 1
-        fine_after = {(1, 3): 0, (1, 6): 1, (last_w, 3): 2}
+        groups = PART // P
+        half = groups // 2
+        fine_after = {(1, 2): 0, (1, 4): 1, (1, 6): 2, (last_w, 4): 3}
         for w in range(WINDOWS):
-            for c in range(PART // P):
+            for c in range(groups):
                 q_group(w, c)
                 if w > 0 and c == Q_LAG - 1:
-                    q_back(w - 1, 0)
-                    q_back(w - 1, 1)
+                    q_back(w - 1, 0, half)
+                    q_back(w - 1, half, half)
                     q_store(w - 1, 0, PART // HEAD)
                 if (w, c) in fine_after:
                     kv_fine(last_w, UNITS - 1, fine_after[(w, c)])
-                if w == last_w and c == BANK // P + Q_LAG - 1:
-                    q_back(w, 0)
+                if w == last_w and c == half + Q_LAG - 1:
+                    q_back(w, 0, half)
                     q_store(w, 0, BANK_HEADS)
-        kv_fine(last_w, UNITS - 1, 3)
-        q_back(last_w, 1)
-        q_store(last_w, BANK_HEADS, BANK_HEADS)
+        quarter = half // 2
+        for first in (half, half + quarter):
+            q_back(last_w, first, quarter)
+            q_store(last_w, first * P // HEAD, quarter * P // HEAD)

@@ -35,15 +35,16 @@ def tile_hieramaskunitattention_pa_kernel(
 ):
     nc = tc.nc
     with tc.tile_pool(name="keep", bufs=1) as keep, tc.tile_pool(
-        name="grouped_pool", bufs=2
-    ) as grouped_pool, tc.tile_pool(name="kv_pool", bufs=6) as kv_pool, tc.tile_pool(
-        name="fine_pool", bufs=4
-    ) as fine_pool, tc.tile_pool(name="q_pool", bufs=2) as q_pool, tc.psum_pool(
+        name="grouped_pool", bufs=3
+    ) as grouped_pool, tc.tile_pool(
+        name="regrouped_pool", bufs=2
+    ) as regrouped_pool, tc.tile_pool(name="kv_pool", bufs=6) as kv_pool, tc.psum_pool(
         name="psum", bufs=8
     ) as psum, tc.manual_schedule():
         ones = keep.tile([P, BANK], BF16)
         nc.vector.memset(ones[:], 1.0)
-        b_rows = [keep.tile([P, PART], BF16, name="b_rows_%d" % part) for part in range(3)]
+        b_rows = keep.tile([P, PART], BF16)
+        nc.vector.memset(b_rows[:].bitcast(I32), 0)
         w_scales = [
             keep.tile([P, PASSES, PART], U8, name="w_scales_%d" % part, align_bytes=64)
             for part in range(3)
@@ -51,7 +52,6 @@ def tile_hieramaskunitattention_pa_kernel(
         first_part = PART_ORDER[0]
 
         def zero(part):
-            nc.vector.memset(b_rows[part][:].bitcast(I32), 0)
             nc.vector.memset(w_scales[part][:].bitcast(I32), 0)
 
         zero(first_part)
@@ -99,7 +99,7 @@ def tile_hieramaskunitattention_pa_kernel(
 
         def load_bias(part):
             nc.sync.dma_start(
-                out=b_rows[part][0:1, :],
+                out=b_rows[0:1, :],
                 in_=qkv_b[part * PART : (part + 1) * PART].rearrange("(o n) -> o n", o=1),
             )
 
@@ -111,10 +111,10 @@ def tile_hieramaskunitattention_pa_kernel(
         load_x(1)
 
         def load_part(part):
-            load_scales(part)
-            load_bias(part)
             load_words(part, 0)
             load_words(part, 1)
+            load_bias(part)
+            load_scales(part)
 
         bias = keep.tile([P, CHANNELS], F32)
 
@@ -124,7 +124,7 @@ def tile_hieramaskunitattention_pa_kernel(
                 nc.tensor.matmul(
                     out=bias_ps[:],
                     lhsT=ones[:, 0:P],
-                    rhs=b_rows[part][:, n0 - part * PART : n0 - part * PART + BANK],
+                    rhs=b_rows[:, n0 - part * PART : n0 - part * PART + BANK],
                     start=True,
                     stop=True,
                 )
@@ -234,70 +234,83 @@ def tile_hieramaskunitattention_pa_kernel(
                     )
             kv_store(w, part, local, BANK_HEADS, kv_sb[:])
 
-        def kv_fine(w, c, sub):
-            part = 1 + c // 2
-            local = (c % 2) * BANK + sub * P
-            n0 = part * PART + local
-            heads = P // HEAD
-            fine_sb = fine_pool.tile([P, heads, TILES, HEAD], F32, name="fine_sb")
-            acc = psum.tile([P, BANK], F32, tag="bank")
-            for j in range(TILES):
-                kv_products(acc[:, j * P : (j + 1) * P], w, j, part, local, P)
-            nc.vector.tensor_tensor(
-                out=fine_sb[:],
-                in0=acc[:].rearrange("p (j h d) -> p h j d", j=TILES, d=HEAD),
-                in1=by_head(bias[:, n0 : n0 + P])
-                .unsqueeze(2)
-                .to_broadcast([P, heads, TILES, HEAD]),
-                op=ADD,
-            )
-            kv_store(w, part, local, heads, fine_sb[:])
+        q_codes = [
+            keep.tile([P, PASSES, STRIDES * P], U32, name="q_codes_%d" % w, align_bytes=64)
+            for w in range(WINDOWS)
+        ]
+        q_scales = [
+            keep.tile([P, PASSES, STRIDES * P], U8, name="q_scales_%d" % w, align_bytes=64)
+            for w in range(WINDOWS)
+        ]
+        q_sb = [
+            keep.tile([P, PART // HEAD, HEAD], F32, name="q_sb_%d" % w) for w in range(WINDOWS)
+        ]
+        regrouped = {}
 
-        q_t = {}
+        def regroup(w, strides):
+            if strides[0] == 0:
+                regrouped[w] = regrouped_pool.tile(
+                    [P, PASSES, STRIDES, P, 4], BF16, name="regrouped_x", align_bytes=64
+                )
+            rows = P // STRIDES
+            for s in strides:
+                for g in range(PASSES):
+                    nc.scalar.copy(
+                        out=regrouped[w][:]
+                        .bitcast(F32)[:, g, s]
+                        .rearrange("p (r j) u -> p r j u", j=TILES),
+                        in_=grouped[w][:]
+                        .bitcast(F32)[:, :, g, s * rows : (s + 1) * rows]
+                        .rearrange("p j r u -> p r j u"),
+                    )
 
-        q_sb = {}
+        def quantise_regrouped(w):
+            for g in range(PASSES):
+                nc.vector.quantize_mx(
+                    out=q_codes[w][:, g].bitcast(FP8X4),
+                    scales=q_scales[w][:, g],
+                    in_=regrouped[w][:, g].rearrange("p s t f -> p (s t f)"),
+                )
 
-        def q_group(w, c):
-            if c == 0:
-                q_t[w] = q_pool.tile([P, PART // P, P], F32, name="q_t")
-            acc = psum.tile([P, BANK], F32, tag="bank")
+        def q_products(acc, w, s, local, width):
             for g in range(PASSES):
                 nc.tensor.matmul_mx(
-                    out=acc[:],
-                    lhsT=w_words[0][c * P // BANK][
-                        :, g, 2 * (c * P % BANK) : 2 * (c * P % BANK + P)
+                    out=acc,
+                    lhsT=q_codes[w][:, g, s * P : (s + 1) * P].bitcast(FP8X4),
+                    lhsT_scale=q_scales[w][:, g, s * P : (s + 1) * P],
+                    rhs=w_words[0][local // BANK][
+                        :, g, 2 * (local % BANK) : 2 * (local % BANK + width)
                     ].bitcast(FP4X4),
-                    lhsT_scale=w_scales[0][:, g, c * P : (c + 1) * P],
-                    rhs=x_codes[w][:, g, :].bitcast(FP8X4),
-                    rhs_scale=x_scales[w][:, g, :],
+                    rhs_scale=w_scales[0][:, g, local : local + width],
                     start=(g == 0),
                     stop=(g == PASSES - 1),
                 )
+
+        def q_bank(w, b, s):
+            dest = q_sb[w][:, b * BANK_HEADS : (b + 1) * BANK_HEADS, :]
+            acc = psum.tile([P, BANK], F32, tag="bank")
+            q_products(acc[:], w, s, b * BANK, BANK)
+            if s == 0:
+                nc.scalar.copy(out=dest, in_=by_head(acc[:]))
+            else:
+                nc.vector.tensor_tensor(out=dest, in0=by_head(acc[:]), in1=dest, op=MAX)
+
+        def q_fine(w, pair):
+            acc = psum.tile([P, BANK], F32, tag="bank")
+            for s in range(STRIDES):
+                q_products(acc[:, s * P : (s + 1) * P], w, s, pair * P, P)
             nc.vector.tensor_reduce(
-                out=q_t[w][:, c, :].rearrange("c (r j) -> c r j", j=TILES),
-                in_=acc[:].rearrange("c (j s r) -> c r j s", j=TILES, s=STRIDES),
+                out=q_sb[w][:, 2 * pair : 2 * pair + 2, :],
+                in_=acc[:].rearrange("p (s h d) -> p h d s", s=STRIDES, d=HEAD),
                 axis=mybir.AxisListType.X,
                 op=MAX,
             )
 
-        def q_back(w, first, count):
-            if first == 0:
-                q_sb[w] = q_pool.tile([P, PART // HEAD, HEAD], F32, name="q_sb")
-            dest = q_sb[w][:, first * P // HEAD : (first + count) * P // HEAD, :]
-            bias_b = by_head(bias[:, first * P : (first + count) * P])
-            back = psum.tile([P, BANK], F32, tag="bank")
-            for a in range(count):
-                nc.tensor.transpose(
-                    out=back[:, a * P : (a + 1) * P],
-                    in_=q_t[w][:, first + a, :],
-                    identity=ident[:],
-                )
-            source = by_head(back[:, 0 : count * P])
-            if first == 0 and w < WINDOWS - 1:
-                nc.scalar.copy(out=dest, in_=source)
-                nc.gpsimd.tensor_tensor(out=dest, in0=dest, in1=bias_b, op=ADD)
-            else:
-                nc.vector.tensor_tensor(out=dest, in0=source, in1=bias_b, op=ADD)
+        def q_bias(w, h0, heads, engine):
+            dest = q_sb[w][:, h0 : h0 + heads, :]
+            engine.tensor_tensor(
+                out=dest, in0=dest, in1=by_head(bias[:, h0 * HEAD : (h0 + heads) * HEAD]), op=ADD
+            )
 
         def q_store(w, h0, heads):
             nc.sync.dma_start(
@@ -329,28 +342,38 @@ def tile_hieramaskunitattention_pa_kernel(
             if w == 0:
                 zero(PART_ORDER[2])
                 load_part(PART_ORDER[2])
+            if w > 0:
+                quantise_regrouped(w - 1)
             kv_unit(w, 2)
             if not last:
                 for j in range(TILES):
                     quantise_tile(w + 1, j)
-                kv_unit(w, 3)
-        last_w = WINDOWS - 1
-        groups = PART // P
-        half = groups // 2
-        fine_after = {(1, 2): 0, (1, 4): 1, (1, 6): 2, (last_w, 4): 3}
+            regroup(w, range(2))
+            kv_unit(w, 3)
+            regroup(w, range(2, 4))
+        quantise_regrouped(WINDOWS - 1)
         for w in range(WINDOWS):
-            for c in range(groups):
-                q_group(w, c)
-                if w > 0 and c == Q_LAG - 1:
-                    q_back(w - 1, 0, half)
-                    q_back(w - 1, half, half)
-                    q_store(w - 1, 0, PART // HEAD)
-                if (w, c) in fine_after:
-                    kv_fine(last_w, UNITS - 1, fine_after[(w, c)])
-                if w == last_w and c == half + Q_LAG - 1:
-                    q_back(w, 0, half)
-                    q_store(w, 0, BANK_HEADS)
-        quarter = half // 2
-        for first in (half, half + quarter):
-            q_back(last_w, first, quarter)
-            q_store(last_w, first * P // HEAD, quarter * P // HEAD)
+            last = w == WINDOWS - 1
+            if not last:
+                for s in range(STRIDES):
+                    for b in range(2):
+                        q_bank(w, b, s)
+                for b in range(2):
+                    q_bias(w, b * BANK_HEADS, BANK_HEADS, nc.gpsimd)
+                q_store(w, 0, PART // HEAD)
+            else:
+                q_bank(w, 0, 0)
+                q_fine(w, 4)
+                q_bank(w, 0, 1)
+                q_bias(w, 8, 2, nc.vector)
+                q_bank(w, 0, 2)
+                q_fine(w, 5)
+                q_bank(w, 0, 3)
+                q_bias(w, 0, BANK_HEADS, nc.gpsimd)
+                q_bias(w, 10, 2, nc.vector)
+                q_store(w, 8, 4)
+                q_fine(w, 6)
+                q_fine(w, 7)
+                q_store(w, 0, BANK_HEADS)
+                q_bias(w, 12, 4, nc.vector)
+                q_store(w, 12, 4)

@@ -360,20 +360,20 @@ def tile_hieramaskunitattention_pa_kernel(
                         q_bank(w, b, s)
                 for b in range(2):
                     q_bias(w, b * BANK_HEADS, BANK_HEADS, nc.gpsimd)
-                q_store(w, 0, PART // HEAD)
+                    q_store(w, b * BANK_HEADS, BANK_HEADS)
             else:
                 q_bank(w, 0, 0)
                 q_fine(w, 4)
                 q_bank(w, 0, 1)
-                q_bias(w, 8, 2, nc.vector)
-                q_bank(w, 0, 2)
                 q_fine(w, 5)
+                q_bias(w, 8, 4, nc.gpsimd)
+                q_store(w, 8, 4)
+                q_bank(w, 0, 2)
                 q_bank(w, 0, 3)
                 q_bias(w, 0, BANK_HEADS, nc.gpsimd)
-                q_bias(w, 10, 2, nc.vector)
-                q_store(w, 8, 4)
-                q_fine(w, 6)
-                q_fine(w, 7)
                 q_store(w, 0, BANK_HEADS)
-                q_bias(w, 12, 4, nc.vector)
+                q_fine(w, 6)
+                q_bias(w, 12, 2, nc.gpsimd)
+                q_fine(w, 7)
+                q_bias(w, 14, 2, nc.gpsimd)
                 q_store(w, 12, 4)

import concourse.mybir as mybir
from concourse.masks import make_identity

F32 = mybir.dt.float32
BF16 = mybir.dt.bfloat16
I32 = mybir.dt.int32
U32 = mybir.dt.uint32
U8 = mybir.dt.uint8
FP8X4 = mybir.dt.float8_e4m3fn_x4
FP4X4 = mybir.dt.float4_e2m1fn_x4
ADD = mybir.AluOpType.add
MAX = mybir.AluOpType.max

P = 128
TOKENS, K, CHANNELS = 1536, 1024, 3072
WINDOWS = 3
TILES = 4
PASSES = 2
HEAD = 64
BANK = 512
BANK_HEADS = BANK // HEAD
PART = 1024
UNITS = 2 * PART // BANK
STRIDES = 4
TWO_STEP_TILE = 1
PART_ORDER = (1, 2, 0)
WARM_UP = (4, 1, 1, 0)
Q_LAG = 2

FLOPS = 2 * TOKENS * K * CHANNELS


def tile_hieramaskunitattention_pa_kernel(
    tc, embeddings, qkv_w_words, qkv_w_scales, qkv_b, out_0, out_1, out_2
):
    nc = tc.nc
    with tc.tile_pool(name="keep", bufs=1) as keep, tc.tile_pool(
        name="grouped_pool", bufs=3
    ) as grouped_pool, tc.tile_pool(
        name="regrouped_pool", bufs=2
    ) as regrouped_pool, tc.tile_pool(name="kv_pool", bufs=6) as kv_pool, tc.psum_pool(
        name="psum", bufs=8
    ) as psum, tc.manual_schedule():
        ones = keep.tile([P, BANK], BF16)
        nc.vector.memset(ones[:], 1.0)
        b_rows = keep.tile([P, PART], BF16)
        nc.vector.memset(b_rows[:].bitcast(I32), 0)
        w_scales = [
            keep.tile([P, PASSES, PART], U8, name="w_scales_%d" % part, align_bytes=64)
            for part in range(3)
        ]
        first_part = PART_ORDER[0]

        def zero(part):
            nc.vector.memset(w_scales[part][:].bitcast(I32), 0)

        zero(first_part)
        ident = keep.tile([P, P], F32)
        make_identity(nc, ident[:])
        warm = keep.tile([P, 1], BF16)
        nc.scalar.copy(out=warm[:], in_=ones[:, 0:1])

        x_view = embeddings[0].rearrange("(p j w) k -> w j p k", j=TILES, w=WINDOWS)
        x_sb = [
            [keep.tile([P, K], BF16, name="x_%d_%d" % (w, j)) for j in range(TILES)]
            for w in range(WINDOWS)
        ]
        words_view = qkv_w_words.bitcast(I32)
        w_words = [
            [
                keep.tile(
                    [P, PASSES, 2 * BANK], U8, name="w_words_%d_%d" % (part, b), align_bytes=64
                )
                for b in range(PART // BANK)
            ]
            for part in range(3)
        ]

        def load_x(w):
            for j in range(TILES):
                nc.sync.dma_start(out=x_sb[w][j][:], in_=x_view[w, j])

        def load_words(part, b):
            first = (part * PART + b * BANK) // 2
            nc.sync.dma_start(
                out=w_words[part][b][:].bitcast(I32),
                in_=words_view[:, :, first : first + BANK // 2].rearrange("g p n -> p g n"),
            )

        scales_view = qkv_w_scales.bitcast(I32)

        def load_scales(part):
            cols = slice(part * PART // 4, (part + 1) * PART // 4)
            for r in range(4):
                nc.sync.dma_start(
                    out=w_scales[part][:].bitcast(I32)[r:P:32],
                    in_=scales_view[:, r:16:4, cols].rearrange("g q n -> q g n"),
                )

        def load_bias(part):
            nc.sync.dma_start(
                out=b_rows[0:1, :],
                in_=qkv_b[part * PART : (part + 1) * PART].rearrange("(o n) -> o n", o=1),
            )

        load_x(0)
        load_bias(PART_ORDER[0])
        load_words(PART_ORDER[0], 0)
        load_scales(PART_ORDER[0])
        load_words(PART_ORDER[0], 1)
        load_x(1)

        def load_part(part):
            load_words(part, 0)
            load_words(part, 1)
            load_bias(part)
            load_scales(part)

        bias = keep.tile([P, CHANNELS], F32)

        def spread_bias(part):
            for n0 in range(part * PART, (part + 1) * PART, BANK):
                bias_ps = psum.tile([P, BANK], F32, tag="bank")
                nc.tensor.matmul(
                    out=bias_ps[:],
                    lhsT=ones[:, 0:P],
                    rhs=b_rows[:, n0 - part * PART : n0 - part * PART + BANK],
                    start=True,
                    stop=True,
                )
                nc.scalar.copy(out=bias[:, n0 : n0 + BANK], in_=bias_ps[:])

        def warm_up(count):
            busy = psum.tile([P, BANK], F32, tag="bank")
            for r in range(count):
                nc.tensor.matmul(
                    out=busy[:], lhsT=ones[:, 0:P], rhs=ones[:], start=True, stop=True
                )

        def by_head(ap):
            return ap.rearrange("p (h d) -> p h d", d=HEAD)

        x_codes = [
            keep.tile([P, PASSES, TILES * P], U32, name="x_codes_%d" % w, align_bytes=64)
            for w in range(WINDOWS)
        ]
        x_scales = [
            keep.tile([P, PASSES, TILES * P], U8, name="x_scales_%d" % w, align_bytes=64)
            for w in range(WINDOWS)
        ]
        grouped = {}
        x_sorted = [
            [keep.tile([P, K // 2], F32, name="x_sorted_%d_%d" % (w, j)) for j in range(TILES)]
            for w in range(WINDOWS)
        ]

        def sort_words(w, j):
            copy = nc.vector.tensor_copy if w == 0 else nc.scalar.copy
            copy(
                out=x_sorted[w][j][:].rearrange("t (g u p) -> t g u p", g=PASSES, u=2),
                in_=x_sb[w][j][:].bitcast(F32).rearrange("t (g p u) -> t g u p", g=PASSES, u=2),
            )

        def transpose_tile(w, j):
            if j == 0:
                grouped[w] = grouped_pool.tile(
                    [P, TILES, PASSES, P, 4], BF16, name="grouped", align_bytes=64
                )
            xt = psum.tile([P, BANK], F32, tag="bank")
            for a in range(BANK // P):
                nc.tensor.transpose(
                    out=xt[:, a * P : (a + 1) * P],
                    in_=x_sorted[w][j][:, a * P : (a + 1) * P],
                    identity=ident[:],
                )
            nc.scalar.copy(
                out=grouped[w][:].bitcast(F32)[:, j],
                in_=xt[:].rearrange("p (g u t) -> p g t u", g=PASSES, u=2),
            )

        def quantise_tile(w, j):
            for g in range(PASSES):
                nc.vector.quantize_mx(
                    out=x_codes[w][:, g, j * P : (j + 1) * P].bitcast(FP8X4),
                    scales=x_scales[w][:, g, j * P : (j + 1) * P],
                    in_=grouped[w][:, j, g].rearrange("p t f -> p (t f)"),
                )

        def kv_products(acc, w, j, part, local, width):
            n0 = part * PART + local
            for g in range(PASSES):
                nc.tensor.matmul_mx(
                    out=acc,
                    lhsT=x_codes[w][:, g, j * P : (j + 1) * P].bitcast(FP8X4),
                    lhsT_scale=x_scales[w][:, g, j * P : (j + 1) * P],
                    rhs=w_words[part][local // BANK][
                        :, g, 2 * (local % BANK) : 2 * (local % BANK + width)
                    ].bitcast(FP4X4),
                    rhs_scale=w_scales[part][:, g, local : local + width],
                    start=(g == 0),
                    stop=(g == PASSES - 1),
                )

        def kv_store(w, part, local, heads, tile_sb):
            dest = out_1 if part == 1 else out_2
            h0 = local // HEAD
            nc.sync.dma_start(
                out=dest[0, h0 : h0 + heads, w].rearrange("h (p j) d -> p h (j d)", j=TILES),
                in_=tile_sb.rearrange("p h j d -> p h (j d)"),
            )

        def kv_unit(w, c):
            part = 1 + c // 2
            local = (c % 2) * BANK
            n0 = part * PART + local
            kv_sb = kv_pool.tile([P, BANK_HEADS, TILES, HEAD], F32, name="kv_sb")
            for j in range(TILES):
                acc = psum.tile([P, BANK], F32, tag="bank")
                kv_products(acc[:], w, j, part, local, BANK)
                if j == TWO_STEP_TILE:
                    nc.scalar.copy(out=kv_sb[:, :, j, :], in_=by_head(acc[:]))
                    nc.gpsimd.tensor_tensor(
                        out=kv_sb[:, :, j, :],
                        in0=kv_sb[:, :, j, :],
                        in1=by_head(bias[:, n0 : n0 + BANK]),
                        op=ADD,
                    )
                else:
                    nc.vector.tensor_tensor(
                        out=kv_sb[:, :, j, :],
                        in0=by_head(acc[:]),
                        in1=by_head(bias[:, n0 : n0 + BANK]),
                        op=ADD,
                    )
            kv_store(w, part, local, BANK_HEADS, kv_sb[:])

        q_codes = [
            keep.tile([P, PASSES, STRIDES * P], U32, name="q_codes_%d" % w, align_bytes=64)
            for w in range(WINDOWS)
        ]
        q_scales = [
            keep.tile([P, PASSES, STRIDES * P], U8, name="q_scales_%d" % w, align_bytes=64)
            for w in range(WINDOWS)
        ]
        q_sb = [
            keep.tile([P, PART // HEAD, HEAD], F32, name="q_sb_%d" % w) for w in range(WINDOWS)
        ]
        regrouped = {}

        def regroup(w, strides):
            if strides[0] == 0:
                regrouped[w] = regrouped_pool.tile(
                    [P, PASSES, STRIDES, P, 4], BF16, name="regrouped_x", align_bytes=64
                )
            rows = P // STRIDES
            for s in strides:
                for g in range(PASSES):
                    nc.scalar.copy(
                        out=regrouped[w][:]
                        .bitcast(F32)[:, g, s]
                        .rearrange("p (r j) u -> p r j u", j=TILES),
                        in_=grouped[w][:]
                        .bitcast(F32)[:, :, g, s * rows : (s + 1) * rows]
                        .rearrange("p j r u -> p r j u"),
                    )

        def quantise_regrouped(w):
            for g in range(PASSES):
                nc.vector.quantize_mx(
                    out=q_codes[w][:, g].bitcast(FP8X4),
                    scales=q_scales[w][:, g],
                    in_=regrouped[w][:, g].rearrange("p s t f -> p (s t f)"),
                )

        def q_products(acc, w, s, local, width):
            for g in range(PASSES):
                nc.tensor.matmul_mx(
                    out=acc,
                    lhsT=q_codes[w][:, g, s * P : (s + 1) * P].bitcast(FP8X4),
                    lhsT_scale=q_scales[w][:, g, s * P : (s + 1) * P],
                    rhs=w_words[0][local // BANK][
                        :, g, 2 * (local % BANK) : 2 * (local % BANK + width)
                    ].bitcast(FP4X4),
                    rhs_scale=w_scales[0][:, g, local : local + width],
                    start=(g == 0),
                    stop=(g == PASSES - 1),
                )

        def q_bank(w, b, s):
            dest = q_sb[w][:, b * BANK_HEADS : (b + 1) * BANK_HEADS, :]
            acc = psum.tile([P, BANK], F32, tag="bank")
            q_products(acc[:], w, s, b * BANK, BANK)
            if s == 0:
                nc.scalar.copy(out=dest, in_=by_head(acc[:]))
            else:
                nc.vector.tensor_tensor(out=dest, in0=by_head(acc[:]), in1=dest, op=MAX)

        def q_fine(w, pair):
            acc = psum.tile([P, BANK], F32, tag="bank")
            for s in range(STRIDES):
                q_products(acc[:, s * P : (s + 1) * P], w, s, pair * P, P)
            nc.vector.tensor_reduce(
                out=q_sb[w][:, 2 * pair : 2 * pair + 2, :],
                in_=acc[:].rearrange("p (s h d) -> p h d s", s=STRIDES, d=HEAD),
                axis=mybir.AxisListType.X,
                op=MAX,
            )

        def q_bias(w, h0, heads, engine):
            dest = q_sb[w][:, h0 : h0 + heads, :]
            engine.tensor_tensor(
                out=dest, in0=dest, in1=by_head(bias[:, h0 * HEAD : (h0 + heads) * HEAD]), op=ADD
            )

        def q_store(w, h0, heads):
            nc.sync.dma_start(
                out=out_0[0, h0 : h0 + heads, w].rearrange("h i d -> i h d"),
                in_=q_sb[w][:, h0 : h0 + heads, :],
            )

        for j in range(TILES):
            sort_words(0, j)
        for j in range(TILES):
            warm_up(WARM_UP[j])
            transpose_tile(0, j)
            quantise_tile(0, j)
        spread_bias(PART_ORDER[0])
        zero(PART_ORDER[1])
        load_part(PART_ORDER[1])
        load_x(2)
        for w in range(WINDOWS):
            last = w == WINDOWS - 1
            kv_unit(w, 0)
            if not last:
                for j in range(TILES):
                    sort_words(w + 1, j)
            kv_unit(w, 1)
            if not last:
                for j in range(TILES):
                    transpose_tile(w + 1, j)
                spread_bias(PART_ORDER[w + 1])
            if w == 0:
                zero(PART_ORDER[2])
                load_part(PART_ORDER[2])
            if w > 0:
                quantise_regrouped(w - 1)
            kv_unit(w, 2)
            if not last:
                for j in range(TILES):
                    quantise_tile(w + 1, j)
            regroup(w, range(2))
            kv_unit(w, 3)
            regroup(w, range(2, 4))
        quantise_regrouped(WINDOWS - 1)
        for w in range(WINDOWS):
            last = w == WINDOWS - 1
            if not last:
                for s in range(STRIDES):
                    for b in range(2):
                        q_bank(w, b, s)
                for b in range(2):
                    q_bias(w, b * BANK_HEADS, BANK_HEADS, nc.gpsimd)
                    q_store(w, b * BANK_HEADS, BANK_HEADS)
            else:
                q_bank(w, 0, 0)
                q_fine(w, 4)
                q_bank(w, 0, 1)
                q_fine(w, 5)
                q_bias(w, 8, 4, nc.gpsimd)
                q_store(w, 8, 4)
                q_bank(w, 0, 2)
                q_bank(w, 0, 3)
                q_bias(w, 0, BANK_HEADS, nc.gpsimd)
                q_store(w, 0, BANK_HEADS)
                q_fine(w, 6)
                q_bias(w, 12, 2, nc.gpsimd)
                q_fine(w, 7)
                q_bias(w, 14, 2, nc.gpsimd)
                q_store(w, 12, 4)
